import numpy as np
import ml_dtypes


def mxq(x, axis, fmt="e4m3"):
    dtype, down = {"e4m3": (ml_dtypes.float8_e4m3fn, 7), "e5m2": (ml_dtypes.float8_e5m2, 14)}[fmt]
    v = np.moveaxis(np.asarray(x, np.float32).astype(ml_dtypes.bfloat16).astype(np.float64), axis, -1)
    blocks = v.reshape(v.shape[:-1] + (-1, 32))
    amax = np.abs(blocks).max(-1, keepdims=True)
    byte = np.maximum(np.where(amax > 0, np.frexp(amax)[1] - 1 + 127, 0) - down, 1)
    scale = np.exp2(byte - 127.0)
    codes = (blocks / scale).astype(np.float32).astype(dtype).astype(np.float64)
    return np.moveaxis((codes * scale).reshape(v.shape), -1, axis)


WIDE = False


def mx_kscale(k):
    if not WIDE:
        return np.ones(k)
    levels = np.array([20, -20, 10, -10, 0])
    a = np.random.permutation(np.resize(levels, k // 512 * 4)).reshape(k // 512, 4)
    idx = np.arange(k)
    return np.exp2(a[idx // 512, idx % 128 // 32])


BF16 = ml_dtypes.bfloat16


def bf(x):
    return np.asarray(x, np.float32).astype(BF16)


def f64(x):
    return np.asarray(x).astype(np.float64)


B, N, F, T, DE, FO, K = 2, 512, 16, 16, 16, 32, 3
C = F * T


def setup_inputs():
    s = mx_kscale(N)
    supports = np.abs(np.random.standard_normal((N, N))) * 0.4 / np.sqrt(N)
    cheb_2 = np.random.standard_normal((N, N)) * 0.8 / np.sqrt(N)
    spatial_attention = np.random.random((B, N, N)) * s[None, None, :]
    x = np.random.standard_normal((B, N, F, T))
    g = np.random.standard_normal((K, B, N, F, T)) * np.exp2(np.random.randint(-12, 1, (K, B, N, 1, 1))) * 8.0
    g = g / s[None, None, :, None, None]
    return {"supports": bf(supports), "cheb_2": bf(cheb_2), "spatial_attention": bf(spatial_attention),
            "x": bf(x), "grad_out": bf(g)}


def reference(supports, cheb_2, spatial_attention, x, grad_out):
    at = f64(spatial_attention)
    g = f64(grad_out).reshape(K, B, N, C)
    r0 = np.diagonal(at, axis1=1, axis2=2)[:, :, None] * g[0]
    r1 = mxq(f64(supports)[None] * at, 2, "e4m3") @ mxq(g[1], 1, "e5m2")
    r2 = mxq(f64(cheb_2)[None] * at, 2, "e4m3") @ mxq(g[2], 1, "e5m2")
    return (r0 + r1 + r2).reshape(B, N, F, T)

@@ -1,0 +1,217 @@
+from contextlib import ExitStack
+
+import concourse.mybir as mybir
+from concourse.masks import make_identity
+
+BF16 = mybir.dt.bfloat16
+F32 = mybir.dt.float32
+U32 = mybir.dt.uint32
+U8 = mybir.dt.uint8
+E4M3_X4 = mybir.dt.float8_e4m3fn_x4
+E5M2_X4 = mybir.dt.float8_e5m2_x4
+MULT = mybir.AluOpType.mult
+ADD = mybir.AluOpType.add
+
+P = 128
+BATCH = 2
+NODES = 512
+CHANNELS = 256
+ORDERS = 2
+ROW_TILES = NODES // P
+PACK = 4
+HALVES = 2
+PAIR = 2
+WORDS = NODES // PAIR
+
+FLOPS = 2 * ORDERS * BATCH * NODES * NODES * CHANNELS
+BYTES = 2 * (ORDERS * NODES * NODES + BATCH * NODES * NODES + 3 * BATCH * NODES * CHANNELS) + 4 * BATCH * NODES * CHANNELS
+
+
+def tile_napl_conv_withsat_pb_s_kernel(tc, supports, cheb_2, spatial_attention, x, grad_out, out):
+    nc = tc.nc
+    with ExitStack() as ctx:
+        keep = ctx.enter_context(tc.tile_pool(name="keep", bufs=1))
+        rows = ctx.enter_context(tc.tile_pool(name="rows", bufs=ROW_TILES))
+        work = ctx.enter_context(tc.tile_pool(name="work", bufs=2))
+        banks = ctx.enter_context(tc.psum_pool(name="banks", bufs=8))
+        ctx.enter_context(tc.manual_schedule())
+
+        identity = keep.tile([P, P], F32)
+        make_identity(nc, identity[:])
+
+        weight_views = [w.rearrange("(p i) m -> p i m", i=ROW_TILES) for w in (supports, cheb_2)]
+        attention_view = spatial_attention.rearrange("b (p i) m -> p b i m", i=ROW_TILES)
+        weight_rows = []
+        attention_rows = []
+        grad_raw = []
+
+        def load_row_tile(i):
+            w_rows = rows.tile([P, ORDERS, NODES], BF16)
+            a_rows = rows.tile([P, BATCH, NODES], BF16)
+            nc.sync.dma_start(out=w_rows[:, 0, :], in_=weight_views[0][:, i, :])
+            nc.sync.dma_start(out=a_rows[:], in_=attention_view[:, :, i, :])
+            nc.sync.dma_start(out=w_rows[:, 1, :], in_=weight_views[1][:, i, :])
+            weight_rows.append(w_rows)
+            attention_rows.append(a_rows)
+
+        def load_grad(k):
+            g_raw = keep.tile([P, BATCH, PACK, CHANNELS], BF16, name="g_raw%d" % k)
+            nc.sync.dma_start(
+                out=g_raw[:].rearrange("p b (u e) c -> p b u (e c)", u=HALVES),
+                in_=grad_out[1 + k].rearrange("b (u p e) f t -> p b u (e f t)", u=HALVES, e=PAIR),
+            )
+            grad_raw.append(g_raw)
+
+        load_row_tile(0)
+        load_row_tile(1)
+        load_grad(0)
+        load_row_tile(2)
+        load_grad(1)
+        load_row_tile(3)
+
+        diagonal_bf16 = keep.tile([P, BATCH, 16], BF16)
+        flat_attention = spatial_attention.rearrange("b n m -> b (n m)")
+        with nc.allow_non_contiguous_dma(reason="the diagonal is 1,024 single elements"):
+            for b in range(BATCH):
+                nc.sync.dma_start(
+                    out=diagonal_bf16[:, b, 0:ROW_TILES],
+                    in_=flat_attention[b, 0 : NODES * NODES : NODES + 1].rearrange("(p i) -> p i", i=ROW_TILES),
+                )
+        grad0 = keep.tile([P, BATCH, ROW_TILES, CHANNELS], BF16)
+        nc.sync.dma_start(
+            out=grad0[:].rearrange("p b i c -> p b (i c)"),
+            in_=grad_out[0].rearrange("b (p i) f t -> p b (i f t)", i=ROW_TILES),
+        )
+        diagonal = keep.tile([P, BATCH, ROW_TILES], F32)
+        nc.gpsimd.tensor_copy(out=diagonal[:], in_=diagonal_bf16[:, :, 0:ROW_TILES])
+
+        prod_codes = keep.tile([P, ROW_TILES, ORDERS * BATCH * P], U32, align_bytes=64)
+        prod_scales = keep.tile([P, ROW_TILES, ORDERS * BATCH * P], U8, align_bytes=64)
+        grad_codes = keep.tile([P, ORDERS, BATCH * CHANNELS], U32, align_bytes=64)
+        grad_scales = keep.tile([P, ORDERS, BATCH * CHANNELS], U8, align_bytes=64)
+        weights_grouped = []
+        attention_turned = []
+        grads_grouped = []
+        sums = []
+
+        def turn(i):
+            w_words = weight_rows[i][:].rearrange("p k m -> p (k m)").bitcast(F32).rearrange("p (k w) -> p k w", k=ORDERS)
+            a_words = attention_rows[i][:].rearrange("p b m -> p (b m)").bitcast(F32).rearrange("p (b w) -> p b w", b=BATCH)
+            w_turned = banks.tile([P, ORDERS, HALVES, P], F32, tag="bank")
+            a_turned = banks.tile([P, HALVES, BATCH, P], F32, tag="bank")
+            w_grouped = work.tile([P, ORDERS, P, HALVES], F32)
+
+            def turn_weights(k):
+                for u in range(HALVES):
+                    nc.tensor.transpose(w_turned[:, k, u, :], w_words[:, k, u * P : (u + 1) * P], identity[:])
+                nc.scalar.copy(out=w_grouped[:, k], in_=w_turned[:, k].rearrange("p u n -> p n u"))
+
+            turn_weights(0)
+            for b in range(BATCH):
+                for u in range(HALVES):
+                    nc.tensor.transpose(a_turned[:, u, b, :], a_words[:, b, u * P : (u + 1) * P], identity[:])
+            turn_weights(1)
+            weights_grouped.append(w_grouped)
+            attention_turned.append(a_turned)
+
+        def quantise_products(i):
+            a_pairs = (
+                attention_turned[i][:]
+                .rearrange("p u b n -> p (u b n)")
+                .bitcast(BF16)
+                .rearrange("p (u b n e) -> p b n u e", u=HALVES, b=BATCH, e=PAIR)
+            )
+            prod = work.tile([P, ORDERS, BATCH, P, PACK], BF16, align_bytes=64)
+            for k in range(ORDERS):
+                w_pairs = (
+                    weights_grouped[i][:, k]
+                    .rearrange("p n u -> p (n u)")
+                    .bitcast(BF16)
+                    .rearrange("p (n u e) -> p n u e", u=HALVES, e=PAIR)
+                    .unsqueeze(1)
+                    .to_broadcast([P, BATCH, P, HALVES, PAIR])
+                )
+                nc.vector.tensor_tensor(
+                    out=prod[:, k].rearrange("p b n (u e) -> p b n u e", u=HALVES),
+                    in0=w_pairs,
+                    in1=a_pairs,
+                    op=MULT,
+                )
+            nc.vector.quantize_mx(
+                out=prod_codes[:, i, :].bitcast(E4M3_X4),
+                scales=prod_scales[:, i, :],
+                in_=prod[:].rearrange("p k b n t -> p (k b n t)"),
+            )
+
+        def regroup_grad(k):
+            g_grouped = keep.tile([P, BATCH, CHANNELS, PACK], BF16, align_bytes=64, name="g_grouped%d" % k)
+            for b in range(BATCH):
+                nc.scalar.copy(
+                    out=g_grouped[:, b].rearrange("p (c r) t -> p c t r", r=4),
+                    in_=grad_raw[k][:, b].rearrange("p t (c r) -> p c t r", r=4),
+                )
+            grads_grouped.append(g_grouped)
+
+        def quantise_grad(k):
+            nc.vector.quantize_mx(
+                out=grad_codes[:, k, :].bitcast(E5M2_X4),
+                scales=grad_scales[:, k, :],
+                in_=grads_grouped[k][:].rearrange("p b c t -> p (b c t)"),
+            )
+
+        def multiply(i, k):
+            if k == 0:
+                for b in range(BATCH):
+                    acc = banks.tile([P, BATCH * CHANNELS], F32, tag="bank")
+                    sums.append(acc)
+            for b in range(BATCH):
+                columns = slice((k * BATCH + b) * P, (k * BATCH + b + 1) * P)
+                nc.tensor.matmul_mx(
+                    out=sums[i * BATCH + b][:],
+                    lhsT=prod_codes[:, i, columns].bitcast(E4M3_X4),
+                    lhsT_scale=prod_scales[:, i, columns],
+                    rhs=grad_codes[:, k, :].bitcast(E5M2_X4),
+                    rhs_scale=grad_scales[:, k, :],
+                    start=(k == 0),
+                    stop=(k == ORDERS - 1),
+                )
+
+        out_view = out.rearrange("b (p i) f t -> p b i (f t)", i=ROW_TILES)
+
+        def finish(i):
+            result = rows.tile([P, BATCH, CHANNELS], F32)
+            for b in range(BATCH):
+                nc.vector.scalar_tensor_tensor(
+                    out=result[:, b, :],
+                    in0=grad0[:, b, i, :],
+                    scalar=diagonal[:, b, i : i + 1],
+                    in1=sums[i * BATCH + b][:, b * CHANNELS : (b + 1) * CHANNELS],
+                    op0=MULT,
+                    op1=ADD,
+                )
+            nc.sync.dma_start(out=out_view[:, :, i, :], in_=result[:])
+
+        turn(0)
+        quantise_products(0)
+        turn(1)
+        quantise_products(1)
+        regroup_grad(0)
+        turn(2)
+        quantise_grad(0)
+        multiply(0, 0)
+        multiply(1, 0)
+        quantise_products(2)
+        regroup_grad(1)
+        turn(3)
+        quantise_grad(1)
+        multiply(2, 0)
+        multiply(0, 1)
+        multiply(1, 1)
+        multiply(2, 1)
+        quantise_products(3)
+        finish(0)
+        finish(1)
+        finish(2)
+        multiply(3, 0)
+        multiply(3, 1)
+        finish(3)

@@ -31,8 +31,6 @@ def tile_napl_conv_withsat_pb_s_kernel(tc, supports, cheb_2, spatial_attention, 
     nc = tc.nc
     with ExitStack() as ctx:
         keep = ctx.enter_context(tc.tile_pool(name="keep", bufs=1))
-        rows = ctx.enter_context(tc.tile_pool(name="rows", bufs=ROW_TILES))
-        work = ctx.enter_context(tc.tile_pool(name="work", bufs=2))
         banks = ctx.enter_context(tc.psum_pool(name="banks", bufs=8))
         ctx.enter_context(tc.manual_schedule())
 
@@ -41,116 +39,102 @@ def tile_napl_conv_withsat_pb_s_kernel(tc, supports, cheb_2, spatial_attention, 
 
         weight_views = [w.rearrange("(p i) m -> p i m", i=ROW_TILES) for w in (supports, cheb_2)]
         attention_view = spatial_attention.rearrange("b (p i) m -> p b i m", i=ROW_TILES)
-        weight_rows = []
-        attention_rows = []
-        grad_raw = []
-
-        def load_row_tile(i):
-            w_rows = rows.tile([P, ORDERS, NODES], BF16)
-            a_rows = rows.tile([P, BATCH, NODES], BF16)
-            nc.sync.dma_start(out=w_rows[:, 0, :], in_=weight_views[0][:, i, :])
-            nc.sync.dma_start(out=a_rows[:], in_=attention_view[:, :, i, :])
-            nc.sync.dma_start(out=w_rows[:, 1, :], in_=weight_views[1][:, i, :])
-            weight_rows.append(w_rows)
-            attention_rows.append(a_rows)
-
-        def load_grad(k):
-            g_raw = keep.tile([P, BATCH, PACK, CHANNELS], BF16, name="g_raw%d" % k)
-            nc.sync.dma_start(
-                out=g_raw[:].rearrange("p b (u e) c -> p b u (e c)", u=HALVES),
-                in_=grad_out[1 + k].rearrange("b (u p e) f t -> p b u (e f t)", u=HALVES, e=PAIR),
-            )
-            grad_raw.append(g_raw)
-
-        load_row_tile(0)
-        load_row_tile(1)
-        load_grad(0)
-        load_row_tile(2)
-        load_grad(1)
-        load_row_tile(3)
-
-        diagonal_bf16 = keep.tile([P, BATCH, 16], BF16)
+        grad_views = [
+            grad_out[1 + k].rearrange("b (u p e) f t -> p b u (e f t)", u=HALVES, e=PAIR) for k in range(ORDERS)
+        ]
         flat_attention = spatial_attention.rearrange("b n m -> b (n m)")
-        with nc.allow_non_contiguous_dma(reason="the diagonal is 1,024 single elements"):
-            for b in range(BATCH):
-                nc.sync.dma_start(
-                    out=diagonal_bf16[:, b, 0:ROW_TILES],
-                    in_=flat_attention[b, 0 : NODES * NODES : NODES + 1].rearrange("(p i) -> p i", i=ROW_TILES),
-                )
-        grad0 = keep.tile([P, BATCH, ROW_TILES, CHANNELS], BF16)
-        nc.sync.dma_start(
-            out=grad0[:].rearrange("p b i c -> p b (i c)"),
-            in_=grad_out[0].rearrange("b (p i) f t -> p b (i f t)", i=ROW_TILES),
-        )
-        diagonal = keep.tile([P, BATCH, ROW_TILES], F32)
-        nc.gpsimd.tensor_copy(out=diagonal[:], in_=diagonal_bf16[:, :, 0:ROW_TILES])
+        out_view = out.rearrange("b (p i) f t -> p b i (f t)", i=ROW_TILES)
 
-        prod_codes = keep.tile([P, ROW_TILES, ORDERS * BATCH * P], U32, align_bytes=64)
-        prod_scales = keep.tile([P, ROW_TILES, ORDERS * BATCH * P], U8, align_bytes=64)
+        weight_rows = [keep.tile([P, ORDERS, NODES], BF16, name="w_rows%d" % i) for i in range(ROW_TILES)]
+        attention_rows = [keep.tile([P, BATCH, NODES], BF16, name="a_rows%d" % i) for i in range(ROW_TILES)]
+        grad_raw = [keep.tile([P, BATCH, PACK, CHANNELS], BF16, name="g_raw%d" % k) for k in range(ORDERS)]
+        grad0 = keep.tile([P, BATCH, ROW_TILES, CHANNELS], BF16)
+        diagonal_bf16 = keep.tile([P, BATCH, 16], BF16)
+        diagonal = keep.tile([P, BATCH, ROW_TILES], F32)
+        weights_grouped = [keep.tile([P, ORDERS, P, HALVES], F32, name="w_grouped%d" % i) for i in range(ROW_TILES)]
+        attention_turned = []
+        products = [
+            keep.tile([P, BATCH, ORDERS, P, PACK], BF16, align_bytes=64, name="prod%d" % i) for i in range(ROW_TILES)
+        ]
+        grads_grouped = [
+            keep.tile([P, BATCH, CHANNELS, PACK], BF16, align_bytes=64, name="g_grouped%d" % k) for k in range(ORDERS)
+        ]
+        prod_codes = keep.tile([P, ROW_TILES, BATCH, ORDERS * P], U32, align_bytes=64)
+        prod_scales = keep.tile([P, ROW_TILES, BATCH, ORDERS * P], U8, align_bytes=64)
         grad_codes = keep.tile([P, ORDERS, BATCH * CHANNELS], U32, align_bytes=64)
         grad_scales = keep.tile([P, ORDERS, BATCH * CHANNELS], U8, align_bytes=64)
-        weights_grouped = []
-        attention_turned = []
-        grads_grouped = []
-        sums = []
+        sums = {}
+        results = [keep.tile([P, BATCH, CHANNELS], F32, name="result%d" % i) for i in range(ROW_TILES)]
+        both = slice(0, BATCH)
+
+        def load_rows(i):
+            for k in range(ORDERS):
+                nc.sync.dma_start(out=weight_rows[i][:, k, :], in_=weight_views[k][:, i, :])
+            nc.sync.dma_start(out=attention_rows[i][:], in_=attention_view[:, :, i, :])
+
+        def load_grad(k, b):
+            nc.sync.dma_start(
+                out=grad_raw[k][:, b].rearrange("p (u e) c -> p u (e c)", u=HALVES),
+                in_=grad_views[k][:, b],
+            )
+
+        def load_diagonal():
+            with nc.allow_non_contiguous_dma(reason="the diagonal is 1,024 single elements"):
+                for b in range(BATCH):
+                    nc.sync.dma_start(
+                        out=diagonal_bf16[:, b, 0:ROW_TILES],
+                        in_=flat_attention[b, 0 : NODES * NODES : NODES + 1].rearrange("(p i) -> p i", i=ROW_TILES),
+                    )
+            nc.gpsimd.tensor_copy(out=diagonal[:], in_=diagonal_bf16[:, :, 0:ROW_TILES])
 
         def turn(i):
             w_words = weight_rows[i][:].rearrange("p k m -> p (k m)").bitcast(F32).rearrange("p (k w) -> p k w", k=ORDERS)
             a_words = attention_rows[i][:].rearrange("p b m -> p (b m)").bitcast(F32).rearrange("p (b w) -> p b w", b=BATCH)
             w_turned = banks.tile([P, ORDERS, HALVES, P], F32, tag="bank")
             a_turned = banks.tile([P, HALVES, BATCH, P], F32, tag="bank")
-            w_grouped = work.tile([P, ORDERS, P, HALVES], F32)
-
-            def turn_weights(k):
+            for k in range(ORDERS):
                 for u in range(HALVES):
                     nc.tensor.transpose(w_turned[:, k, u, :], w_words[:, k, u * P : (u + 1) * P], identity[:])
-                nc.scalar.copy(out=w_grouped[:, k], in_=w_turned[:, k].rearrange("p u n -> p n u"))
-
-            turn_weights(0)
             for b in range(BATCH):
                 for u in range(HALVES):
                     nc.tensor.transpose(a_turned[:, u, b, :], a_words[:, b, u * P : (u + 1) * P], identity[:])
-            turn_weights(1)
-            weights_grouped.append(w_grouped)
+            nc.scalar.copy(out=weights_grouped[i][:], in_=w_turned[:].rearrange("p k u n -> p k n u"))
             attention_turned.append(a_turned)
 
-        def quantise_products(i):
+        def multiply_turned(i, k, samples):
             a_pairs = (
                 attention_turned[i][:]
                 .rearrange("p u b n -> p (u b n)")
                 .bitcast(BF16)
-                .rearrange("p (u b n e) -> p b n u e", u=HALVES, b=BATCH, e=PAIR)
+                .rearrange("p (u b n e) -> p b n u e", u=HALVES, b=BATCH, e=PAIR)[:, samples]
             )
-            prod = work.tile([P, ORDERS, BATCH, P, PACK], BF16, align_bytes=64)
-            for k in range(ORDERS):
-                w_pairs = (
-                    weights_grouped[i][:, k]
-                    .rearrange("p n u -> p (n u)")
-                    .bitcast(BF16)
-                    .rearrange("p (n u e) -> p n u e", u=HALVES, e=PAIR)
-                    .unsqueeze(1)
-                    .to_broadcast([P, BATCH, P, HALVES, PAIR])
-                )
-                nc.vector.tensor_tensor(
-                    out=prod[:, k].rearrange("p b n (u e) -> p b n u e", u=HALVES),
-                    in0=w_pairs,
-                    in1=a_pairs,
-                    op=MULT,
-                )
-            nc.vector.quantize_mx(
-                out=prod_codes[:, i, :].bitcast(E4M3_X4),
-                scales=prod_scales[:, i, :],
-                in_=prod[:].rearrange("p k b n t -> p (k b n t)"),
+            w_pairs = (
+                weights_grouped[i][:, k]
+                .rearrange("p n u -> p (n u)")
+                .bitcast(BF16)
+                .rearrange("p (n u e) -> p n u e", u=HALVES, e=PAIR)
+                .unsqueeze(1)
+                .to_broadcast([P, samples.stop - samples.start, P, HALVES, PAIR])
+            )
+            nc.vector.tensor_tensor(
+                out=products[i][:, samples, k].rearrange("p b n (u e) -> p b n u e", u=HALVES),
+                in0=w_pairs,
+                in1=a_pairs,
+                op=MULT,
             )
 
-        def regroup_grad(k):
-            g_grouped = keep.tile([P, BATCH, CHANNELS, PACK], BF16, align_bytes=64, name="g_grouped%d" % k)
-            for b in range(BATCH):
-                nc.scalar.copy(
-                    out=g_grouped[:, b].rearrange("p (c r) t -> p c t r", r=4),
-                    in_=grad_raw[k][:, b].rearrange("p t (c r) -> p c t r", r=4),
-                )
-            grads_grouped.append(g_grouped)
+        def quantise_products(i, samples):
+            nc.vector.quantize_mx(
+                out=prod_codes[:, i, samples].rearrange("p b n -> p (b n)").bitcast(E4M3_X4),
+                scales=prod_scales[:, i, samples].rearrange("p b n -> p (b n)"),
+                in_=products[i][:, samples].rearrange("p b k n t -> p (b k n t)"),
+            )
+
+        def regroup_grad(k, b):
+            nc.scalar.copy(
+                out=grads_grouped[k][:, b].rearrange("p (c r) t -> p c t r", r=4),
+                in_=grad_raw[k][:, b].rearrange("p t (c r) -> p c t r", r=4),
+            )
 
         def quantise_grad(k):
             nc.vector.quantize_mx(
@@ -159,59 +143,88 @@ def tile_napl_conv_withsat_pb_s_kernel(tc, supports, cheb_2, spatial_attention, 
                 in_=grads_grouped[k][:].rearrange("p b c t -> p (b c t)"),
             )
 
-        def multiply(i, k):
+        def multiply(i, k, b):
             if k == 0:
-                for b in range(BATCH):
-                    acc = banks.tile([P, BATCH * CHANNELS], F32, tag="bank")
-                    sums.append(acc)
-            for b in range(BATCH):
-                columns = slice((k * BATCH + b) * P, (k * BATCH + b + 1) * P)
-                nc.tensor.matmul_mx(
-                    out=sums[i * BATCH + b][:],
-                    lhsT=prod_codes[:, i, columns].bitcast(E4M3_X4),
-                    lhsT_scale=prod_scales[:, i, columns],
-                    rhs=grad_codes[:, k, :].bitcast(E5M2_X4),
-                    rhs_scale=grad_scales[:, k, :],
-                    start=(k == 0),
-                    stop=(k == ORDERS - 1),
-                )
+                acc = banks.tile([P, BATCH * CHANNELS], F32, tag="bank")
+                sums[i, b] = acc
+            columns = slice(k * P, (k + 1) * P)
+            nc.tensor.matmul_mx(
+                out=sums[i, b][:],
+                lhsT=prod_codes[:, i, b, columns].bitcast(E4M3_X4),
+                lhsT_scale=prod_scales[:, i, b, columns],
+                rhs=grad_codes[:, k, :].bitcast(E5M2_X4),
+                rhs_scale=grad_scales[:, k, :],
+                start=(k == 0),
+                stop=(k == ORDERS - 1),
+            )
 
-        out_view = out.rearrange("b (p i) f t -> p b i (f t)", i=ROW_TILES)
+        def finish(i, b):
+            nc.vector.scalar_tensor_tensor(
+                out=results[i][:, b, :],
+                in0=grad0[:, b, i, :],
+                scalar=diagonal[:, b, i : i + 1],
+                in1=sums[i, b][:, b * CHANNELS : (b + 1) * CHANNELS],
+                op0=MULT,
+                op1=ADD,
+            )
 
-        def finish(i):
-            result = rows.tile([P, BATCH, CHANNELS], F32)
+        def store(i, samples):
+            nc.sync.dma_start(out=out_view[:, samples, i, :], in_=results[i][:, samples, :])
+
+        load_rows(0)
+        load_grad(0, 0)
+        load_rows(1)
+        load_grad(0, 1)
+        load_rows(2)
+        load_grad(1, 0)
+        load_grad(1, 1)
+        load_rows(3)
+        load_diagonal()
+        nc.sync.dma_start(
+            out=grad0[:].rearrange("p b i c -> p b (i c)"),
+            in_=grad_out[0].rearrange("b (p i) f t -> p b (i f t)", i=ROW_TILES),
+        )
+
+        def multiply_row_tile(i, samples):
+            for k in range(ORDERS):
+                multiply_turned(i, k, samples)
+
+        def multiply_both(i, k):
             for b in range(BATCH):
-                nc.vector.scalar_tensor_tensor(
-                    out=result[:, b, :],
-                    in0=grad0[:, b, i, :],
-                    scalar=diagonal[:, b, i : i + 1],
-                    in1=sums[i * BATCH + b][:, b * CHANNELS : (b + 1) * CHANNELS],
-                    op0=MULT,
-                    op1=ADD,
-                )
-            nc.sync.dma_start(out=out_view[:, :, i, :], in_=result[:])
+                multiply(i, k, b)
 
         turn(0)
-        quantise_products(0)
+        regroup_grad(0, 0)
+        multiply_row_tile(0, both)
+        quantise_products(0, both)
         turn(1)
-        quantise_products(1)
-        regroup_grad(0)
-        turn(2)
+        regroup_grad(0, 1)
+        multiply_row_tile(1, both)
         quantise_grad(0)
-        multiply(0, 0)
-        multiply(1, 0)
-        quantise_products(2)
-        regroup_grad(1)
-        turn(3)
+        quantise_products(1, both)
+        turn(2)
+        regroup_grad(1, 0)
+        regroup_grad(1, 1)
+        multiply_row_tile(2, both)
+        multiply_both(0, 0)
+        quantise_products(2, both)
         quantise_grad(1)
-        multiply(2, 0)
-        multiply(0, 1)
-        multiply(1, 1)
-        multiply(2, 1)
-        quantise_products(3)
-        finish(0)
-        finish(1)
-        finish(2)
-        multiply(3, 0)
-        multiply(3, 1)
-        finish(3)
+        turn(3)
+        for b in range(BATCH):
+            multiply_row_tile(3, slice(b, b + 1))
+        for b in range(BATCH):
+            quantise_products(3, slice(b, b + 1))
+        multiply_both(1, 0)
+        multiply_both(0, 1)
+        multiply_both(1, 1)
+        multiply_both(2, 0)
+        multiply_both(2, 1)
+        for i in range(ROW_TILES - 1):
+            for b in range(BATCH):
+                finish(i, b)
+            store(i, both)
+        for b in range(BATCH):
+            for k in range(ORDERS):
+                multiply(3, k, b)
+            finish(3, b)
+            store(3, slice(b, b + 1))

@@ -22,6 +22,9 @@ PACK = 4
 HALVES = 2
 PAIR = 2
 WORDS = NODES // PAIR
+GRAD_SLOTS = 5
+GRAD_SLOT = {(0, 0): 1, (1, 0): 2, (0, 1): 3, (1, 1): 4}
+SUM_BANK = {(0, 0): 1, (1, 0): 2, (2, 0): 3, (0, 1): 4, (1, 1): 5, (2, 1): 6, (3, 0): 7, (3, 1): 0}
 
 FLOPS = 2 * ORDERS * BATCH * NODES * NODES * CHANNELS
 BYTES = 2 * (ORDERS * NODES * NODES + BATCH * NODES * NODES + 3 * BATCH * NODES * CHANNELS) + 4 * BATCH * NODES * CHANNELS
@@ -31,7 +34,7 @@ def tile_napl_conv_withsat_pb_s_kernel(tc, supports, cheb_2, spatial_attention, 
     nc = tc.nc
     with ExitStack() as ctx:
         keep = ctx.enter_context(tc.tile_pool(name="keep", bufs=1))
-        banks = ctx.enter_context(tc.psum_pool(name="banks", bufs=8))
+        banks = ctx.enter_context(tc.psum_pool(name="banks", bufs=1))
         ctx.enter_context(tc.manual_schedule())
 
         identity = keep.tile([P, P], F32)
@@ -43,40 +46,58 @@ def tile_napl_conv_withsat_pb_s_kernel(tc, supports, cheb_2, spatial_attention, 
             grad_out[1 + k].rearrange("b (u p e) f t -> p b u (e f t)", u=HALVES, e=PAIR) for k in range(ORDERS)
         ]
         flat_attention = spatial_attention.rearrange("b n m -> b (n m)")
+        grad0_view = grad_out[0].rearrange("b (p i) f t -> p b (i f t)", i=ROW_TILES)
         out_view = out.rearrange("b (p i) f t -> p b i (f t)", i=ROW_TILES)
 
         weight_rows = [keep.tile([P, ORDERS, NODES], BF16, name="w_rows%d" % i) for i in range(ROW_TILES)]
         attention_rows = [keep.tile([P, BATCH, NODES], BF16, name="a_rows%d" % i) for i in range(ROW_TILES)]
-        grad_raw = [keep.tile([P, BATCH, PACK, CHANNELS], BF16, name="g_raw%d" % k) for k in range(ORDERS)]
-        grad0 = keep.tile([P, BATCH, ROW_TILES, CHANNELS], BF16)
+        grad_raw = {
+            (k, b): keep.tile([P, PACK, CHANNELS], BF16, name="g_raw%d%d" % (k, b))
+            for k in range(ORDERS)
+            for b in range(BATCH)
+        }
+        grad0 = [keep.tile([P, ROW_TILES, CHANNELS], BF16, name="grad0_%d" % b) for b in range(BATCH)]
         diagonal_bf16 = keep.tile([P, BATCH, 16], BF16)
         diagonal = keep.tile([P, BATCH, ROW_TILES], F32)
         weights_grouped = [keep.tile([P, ORDERS, P, HALVES], F32, name="w_grouped%d" % i) for i in range(ROW_TILES)]
-        attention_turned = []
         products = [
-            keep.tile([P, BATCH, ORDERS, P, PACK], BF16, align_bytes=64, name="prod%d" % i) for i in range(ROW_TILES)
+            keep.tile([P, ORDERS, BATCH, P, PACK], BF16, align_bytes=64, name="prod%d" % i) for i in range(ROW_TILES)
         ]
-        grads_grouped = [
-            keep.tile([P, BATCH, CHANNELS, PACK], BF16, align_bytes=64, name="g_grouped%d" % k) for k in range(ORDERS)
-        ]
-        prod_codes = keep.tile([P, ROW_TILES, BATCH, ORDERS * P], U32, align_bytes=64)
-        prod_scales = keep.tile([P, ROW_TILES, BATCH, ORDERS * P], U8, align_bytes=64)
-        grad_codes = keep.tile([P, ORDERS, BATCH * CHANNELS], U32, align_bytes=64)
-        grad_scales = keep.tile([P, ORDERS, BATCH * CHANNELS], U8, align_bytes=64)
+        grads_grouped = {
+            (k, b): keep.tile([P, CHANNELS, PACK], BF16, align_bytes=64, name="g_grouped%d%d" % (k, b))
+            for k in range(ORDERS)
+            for b in range(BATCH)
+        }
+        prod_codes = keep.tile([P, ROW_TILES, ORDERS, BATCH * P], U32, align_bytes=64)
+        prod_scales = keep.tile([P, ROW_TILES, ORDERS, BATCH * P], U8, align_bytes=64)
+        grad_codes = keep.tile([P, GRAD_SLOTS, CHANNELS], U32, align_bytes=64)
+        grad_scales = keep.tile([P, GRAD_SLOTS, CHANNELS], U8, align_bytes=64)
+        nc.gpsimd.memset(grad_codes[:, 0, :], 0)
+        nc.gpsimd.memset(grad_scales[:, 0, :], 0)
+        weights_turned = {}
+        attention_turned = {}
         sums = {}
-        results = [keep.tile([P, BATCH, CHANNELS], F32, name="result%d" % i) for i in range(ROW_TILES)]
-        both = slice(0, BATCH)
+        results = [
+            keep.tile([P, ROW_TILES, CHANNELS], F32, name="result%d" % b) for b in range(BATCH)
+        ]
 
-        def load_rows(i):
-            for k in range(ORDERS):
-                nc.sync.dma_start(out=weight_rows[i][:, k, :], in_=weight_views[k][:, i, :])
+        def bank(shape, slot):
+            return banks.tile(shape, F32, tag="bank%d" % slot, name="in_bank%d" % slot)
+
+        def load_weights(i, k):
+            nc.sync.dma_start(out=weight_rows[i][:, k, :], in_=weight_views[k][:, i, :])
+
+        def load_attention(i):
             nc.sync.dma_start(out=attention_rows[i][:], in_=attention_view[:, :, i, :])
 
         def load_grad(k, b):
             nc.sync.dma_start(
-                out=grad_raw[k][:, b].rearrange("p (u e) c -> p u (e c)", u=HALVES),
+                out=grad_raw[k, b][:].rearrange("p (u e) c -> p u (e c)", u=HALVES),
                 in_=grad_views[k][:, b],
             )
+
+        def load_grad0(b):
+            nc.sync.dma_start(out=grad0[b][:].rearrange("p i c -> p (i c)"), in_=grad0_view[:, b])
 
         def load_diagonal():
             with nc.allow_non_contiguous_dma(reason="the diagonal is 1,024 single elements"):
@@ -87,26 +108,34 @@ def tile_napl_conv_withsat_pb_s_kernel(tc, supports, cheb_2, spatial_attention, 
                     )
             nc.gpsimd.tensor_copy(out=diagonal[:], in_=diagonal_bf16[:, :, 0:ROW_TILES])
 
-        def turn(i):
-            w_words = weight_rows[i][:].rearrange("p k m -> p (k m)").bitcast(F32).rearrange("p (k w) -> p k w", k=ORDERS)
-            a_words = attention_rows[i][:].rearrange("p b m -> p (b m)").bitcast(F32).rearrange("p (b w) -> p b w", b=BATCH)
-            w_turned = banks.tile([P, ORDERS, HALVES, P], F32, tag="bank")
-            a_turned = banks.tile([P, HALVES, BATCH, P], F32, tag="bank")
-            for k in range(ORDERS):
+        def turn_weights(i, orders, slot):
+            words = weight_rows[i][:].rearrange("p k m -> p (k m)").bitcast(F32).rearrange("p (k w) -> p k w", k=ORDERS)
+            turned = bank([P, len(orders), HALVES, P], slot)
+            for j, k in enumerate(orders):
                 for u in range(HALVES):
-                    nc.tensor.transpose(w_turned[:, k, u, :], w_words[:, k, u * P : (u + 1) * P], identity[:])
+                    nc.tensor.transpose(turned[:, j, u, :], words[:, k, u * P : (u + 1) * P], identity[:])
+            weights_turned[i, orders] = turned
+
+        def turn_attention(i, slot):
+            words = attention_rows[i][:].rearrange("p b m -> p (b m)").bitcast(F32).rearrange("p (b w) -> p b w", b=BATCH)
+            turned = bank([P, HALVES, BATCH, P], slot)
             for b in range(BATCH):
                 for u in range(HALVES):
-                    nc.tensor.transpose(a_turned[:, u, b, :], a_words[:, b, u * P : (u + 1) * P], identity[:])
-            nc.scalar.copy(out=weights_grouped[i][:], in_=w_turned[:].rearrange("p k u n -> p k n u"))
-            attention_turned.append(a_turned)
+                    nc.tensor.transpose(turned[:, u, b, :], words[:, b, u * P : (u + 1) * P], identity[:])
+            attention_turned[i] = turned
 
-        def multiply_turned(i, k, samples):
+        def group_weights(i, orders):
+            nc.scalar.copy(
+                out=weights_grouped[i][:, orders[0] : orders[-1] + 1],
+                in_=weights_turned[i, orders][:].rearrange("p k u n -> p k n u"),
+            )
+
+        def multiply_turned(i, k):
             a_pairs = (
                 attention_turned[i][:]
                 .rearrange("p u b n -> p (u b n)")
                 .bitcast(BF16)
-                .rearrange("p (u b n e) -> p b n u e", u=HALVES, b=BATCH, e=PAIR)[:, samples]
+                .rearrange("p (u b n e) -> p b n u e", u=HALVES, b=BATCH, e=PAIR)
             )
             w_pairs = (
                 weights_grouped[i][:, k]
@@ -114,117 +143,147 @@ def tile_napl_conv_withsat_pb_s_kernel(tc, supports, cheb_2, spatial_attention, 
                 .bitcast(BF16)
                 .rearrange("p (n u e) -> p n u e", u=HALVES, e=PAIR)
                 .unsqueeze(1)
-                .to_broadcast([P, samples.stop - samples.start, P, HALVES, PAIR])
+                .to_broadcast([P, BATCH, P, HALVES, PAIR])
             )
             nc.vector.tensor_tensor(
-                out=products[i][:, samples, k].rearrange("p b n (u e) -> p b n u e", u=HALVES),
+                out=products[i][:, k].rearrange("p b n (u e) -> p b n u e", u=HALVES),
                 in0=w_pairs,
                 in1=a_pairs,
                 op=MULT,
             )
 
-        def quantise_products(i, samples):
+        def quantise_products(i, k):
             nc.vector.quantize_mx(
-                out=prod_codes[:, i, samples].rearrange("p b n -> p (b n)").bitcast(E4M3_X4),
-                scales=prod_scales[:, i, samples].rearrange("p b n -> p (b n)"),
-                in_=products[i][:, samples].rearrange("p b k n t -> p (b k n t)"),
+                out=prod_codes[:, i, k, :].bitcast(E4M3_X4),
+                scales=prod_scales[:, i, k, :],
+                in_=products[i][:, k].rearrange("p b n t -> p (b n t)"),
             )
 
         def regroup_grad(k, b):
             nc.scalar.copy(
-                out=grads_grouped[k][:, b].rearrange("p (c r) t -> p c t r", r=4),
-                in_=grad_raw[k][:, b].rearrange("p t (c r) -> p c t r", r=4),
+                out=grads_grouped[k, b][:].rearrange("p (c r) t -> p c t r", r=4),
+                in_=grad_raw[k, b][:].rearrange("p t (c r) -> p c t r", r=4),
             )
 
-        def quantise_grad(k):
+        def quantise_grad(k, b):
+            slot = GRAD_SLOT[k, b]
             nc.vector.quantize_mx(
-                out=grad_codes[:, k, :].bitcast(E5M2_X4),
-                scales=grad_scales[:, k, :],
-                in_=grads_grouped[k][:].rearrange("p b c t -> p (b c t)"),
+                out=grad_codes[:, slot, :].bitcast(E5M2_X4),
+                scales=grad_scales[:, slot, :],
+                in_=grads_grouped[k, b][:].rearrange("p c t -> p (c t)"),
             )
 
-        def multiply(i, k, b):
+        def multiply(i, b, k):
             if k == 0:
-                acc = banks.tile([P, BATCH * CHANNELS], F32, tag="bank")
+                acc = bank([P, 2 * CHANNELS], SUM_BANK[i, b])
                 sums[i, b] = acc
-            columns = slice(k * P, (k + 1) * P)
+            slot = GRAD_SLOT[k, b]
+            columns = slice(b * P, (b + 1) * P)
             nc.tensor.matmul_mx(
                 out=sums[i, b][:],
-                lhsT=prod_codes[:, i, b, columns].bitcast(E4M3_X4),
-                lhsT_scale=prod_scales[:, i, b, columns],
-                rhs=grad_codes[:, k, :].bitcast(E5M2_X4),
-                rhs_scale=grad_scales[:, k, :],
+                lhsT=prod_codes[:, i, k, columns].bitcast(E4M3_X4),
+                lhsT_scale=prod_scales[:, i, k, columns],
+                rhs=grad_codes[:, slot - 1 : slot + 1, :].rearrange("p s c -> p (s c)").bitcast(E5M2_X4),
+                rhs_scale=grad_scales[:, slot - 1 : slot + 1, :].rearrange("p s c -> p (s c)"),
                 start=(k == 0),
                 stop=(k == ORDERS - 1),
             )
 
         def finish(i, b):
             nc.vector.scalar_tensor_tensor(
-                out=results[i][:, b, :],
-                in0=grad0[:, b, i, :],
+                out=results[b][:, i, :],
+                in0=grad0[b][:, i, :],
                 scalar=diagonal[:, b, i : i + 1],
-                in1=sums[i, b][:, b * CHANNELS : (b + 1) * CHANNELS],
+                in1=sums[i, b][:, CHANNELS:],
                 op0=MULT,
                 op1=ADD,
             )
 
-        def store(i, samples):
-            nc.sync.dma_start(out=out_view[:, samples, i, :], in_=results[i][:, samples, :])
+        def store(b, first, last):
+            nc.sync.dma_start(out=out_view[:, b, first : last + 1, :], in_=results[b][:, first : last + 1, :])
 
-        load_rows(0)
+        load_weights(0, 0)
+        load_attention(0)
+        load_weights(0, 1)
+        for k in range(ORDERS):
+            load_weights(1, k)
+        load_attention(1)
         load_grad(0, 0)
-        load_rows(1)
-        load_grad(0, 1)
-        load_rows(2)
+        for k in range(ORDERS):
+            load_weights(2, k)
+        load_attention(2)
         load_grad(1, 0)
+        load_grad(0, 1)
+        for k in range(ORDERS):
+            load_weights(3, k)
+        load_attention(3)
         load_grad(1, 1)
-        load_rows(3)
         load_diagonal()
-        nc.sync.dma_start(
-            out=grad0[:].rearrange("p b i c -> p b (i c)"),
-            in_=grad_out[0].rearrange("b (p i) f t -> p b (i f t)", i=ROW_TILES),
-        )
+        load_grad0(0)
+        load_grad0(1)
 
-        def multiply_row_tile(i, samples):
-            for k in range(ORDERS):
-                multiply_turned(i, k, samples)
+        turn_weights(0, (0,), 0)
+        turn_attention(0, 1)
+        turn_weights(0, (1,), 2)
+        group_weights(0, (0,))
+        group_weights(0, (1,))
+        multiply_turned(0, 0)
+        multiply_turned(0, 1)
+        quantise_products(0, 0)
+        quantise_products(0, 1)
 
-        def multiply_both(i, k):
-            for b in range(BATCH):
-                multiply(i, k, b)
-
-        turn(0)
+        turn_weights(1, (0, 1), 3)
+        turn_attention(1, 4)
+        group_weights(1, (0, 1))
         regroup_grad(0, 0)
-        multiply_row_tile(0, both)
-        quantise_products(0, both)
-        turn(1)
-        regroup_grad(0, 1)
-        multiply_row_tile(1, both)
-        quantise_grad(0)
-        quantise_products(1, both)
-        turn(2)
+        multiply_turned(1, 0)
+        multiply_turned(1, 1)
+        quantise_products(1, 0)
+        quantise_products(1, 1)
+        quantise_grad(0, 0)
+
+        turn_weights(2, (0, 1), 5)
+        turn_attention(2, 6)
+        group_weights(2, (0, 1))
         regroup_grad(1, 0)
+        regroup_grad(0, 1)
+        multiply_turned(2, 0)
+        multiply_turned(2, 1)
+        quantise_products(2, 0)
+        quantise_products(2, 1)
+        quantise_grad(1, 0)
+        quantise_grad(0, 1)
+
+        turn_weights(3, (0, 1), 7)
+        turn_attention(3, 0)
+        group_weights(3, (0, 1))
         regroup_grad(1, 1)
-        multiply_row_tile(2, both)
-        multiply_both(0, 0)
-        quantise_products(2, both)
-        quantise_grad(1)
-        turn(3)
-        for b in range(BATCH):
-            multiply_row_tile(3, slice(b, b + 1))
-        for b in range(BATCH):
-            quantise_products(3, slice(b, b + 1))
-        multiply_both(1, 0)
-        multiply_both(0, 1)
-        multiply_both(1, 1)
-        multiply_both(2, 0)
-        multiply_both(2, 1)
+        for k in range(ORDERS):
+            for i in range(ROW_TILES - 1):
+                multiply(i, 0, k)
         for i in range(ROW_TILES - 1):
-            for b in range(BATCH):
-                finish(i, b)
-            store(i, both)
+            multiply(i, 1, 0)
+        multiply_turned(3, 0)
+        multiply_turned(3, 1)
+        quantise_products(3, 0)
+        quantise_grad(1, 1)
+        quantise_products(3, 1)
         for b in range(BATCH):
-            for k in range(ORDERS):
-                multiply(3, k, b)
+            multiply(3, b, 0)
+        for i in range(ROW_TILES - 1):
+            multiply(i, 1, 1)
+        for b in range(BATCH):
+            multiply(3, b, 1)
+        finish(0, 0)
+        finish(1, 0)
+        store(0, 0, 1)
+        finish(2, 0)
+        store(0, 2, 2)
+        finish(0, 1)
+        finish(1, 1)
+        store(1, 0, 1)
+        finish(2, 1)
+        store(1, 2, 2)
+        for b in range(BATCH):
             finish(3, b)
-            store(3, slice(b, b + 1))
+            store(b, 3, 3)

@@ -21,10 +21,9 @@ ROW_TILES = NODES // P
 PACK = 4
 HALVES = 2
 PAIR = 2
-WORDS = NODES // PAIR
 GRAD_SLOTS = 5
 GRAD_SLOT = {(0, 0): 1, (1, 0): 2, (0, 1): 3, (1, 1): 4}
-SUM_BANK = {(0, 0): 1, (1, 0): 2, (2, 0): 3, (0, 1): 4, (1, 1): 5, (2, 1): 6, (3, 0): 7, (3, 1): 0}
+SUM_BANK = {(0, 0): 1, (1, 0): 3, (2, 0): 4, (0, 1): 5, (1, 1): 6, (2, 1): 7, (3, 0): 0, (3, 1): 2}
 
 FLOPS = 2 * ORDERS * BATCH * NODES * NODES * CHANNELS
 BYTES = 2 * (ORDERS * NODES * NODES + BATCH * NODES * NODES + 3 * BATCH * NODES * CHANNELS) + 4 * BATCH * NODES * CHANNELS
@@ -87,8 +86,8 @@ def tile_napl_conv_withsat_pb_s_kernel(tc, supports, cheb_2, spatial_attention, 
         def load_weights(i, k):
             nc.sync.dma_start(out=weight_rows[i][:, k, :], in_=weight_views[k][:, i, :])
 
-        def load_attention(i):
-            nc.sync.dma_start(out=attention_rows[i][:], in_=attention_view[:, :, i, :])
+        def load_attention(i, samples=slice(0, BATCH)):
+            nc.sync.dma_start(out=attention_rows[i][:, samples], in_=attention_view[:, samples, i, :])
 
         def load_grad(k, b):
             nc.sync.dma_start(
@@ -116,13 +115,13 @@ def tile_napl_conv_withsat_pb_s_kernel(tc, supports, cheb_2, spatial_attention, 
                     nc.tensor.transpose(turned[:, j, u, :], words[:, k, u * P : (u + 1) * P], identity[:])
             weights_turned[i, orders] = turned
 
-        def turn_attention(i, slot):
+        def turn_attention(i, samples, slot):
             words = attention_rows[i][:].rearrange("p b m -> p (b m)").bitcast(F32).rearrange("p (b w) -> p b w", b=BATCH)
-            turned = bank([P, HALVES, BATCH, P], slot)
-            for b in range(BATCH):
+            turned = bank([P, HALVES, len(samples), P], slot)
+            for j, b in enumerate(samples):
                 for u in range(HALVES):
-                    nc.tensor.transpose(turned[:, u, b, :], words[:, b, u * P : (u + 1) * P], identity[:])
-            attention_turned[i] = turned
+                    nc.tensor.transpose(turned[:, u, j, :], words[:, b, u * P : (u + 1) * P], identity[:])
+            attention_turned[i, samples] = turned
 
         def group_weights(i, orders):
             nc.scalar.copy(
@@ -130,12 +129,12 @@ def tile_napl_conv_withsat_pb_s_kernel(tc, supports, cheb_2, spatial_attention, 
                 in_=weights_turned[i, orders][:].rearrange("p k u n -> p k n u"),
             )
 
-        def multiply_turned(i, k):
+        def multiply_turned(i, k, samples=(0, 1)):
             a_pairs = (
-                attention_turned[i][:]
+                attention_turned[i, samples][:]
                 .rearrange("p u b n -> p (u b n)")
                 .bitcast(BF16)
-                .rearrange("p (u b n e) -> p b n u e", u=HALVES, b=BATCH, e=PAIR)
+                .rearrange("p (u b n e) -> p b n u e", u=HALVES, b=len(samples), e=PAIR)
             )
             w_pairs = (
                 weights_grouped[i][:, k]
@@ -143,10 +142,10 @@ def tile_napl_conv_withsat_pb_s_kernel(tc, supports, cheb_2, spatial_attention, 
                 .bitcast(BF16)
                 .rearrange("p (n u e) -> p n u e", u=HALVES, e=PAIR)
                 .unsqueeze(1)
-                .to_broadcast([P, BATCH, P, HALVES, PAIR])
+                .to_broadcast([P, len(samples), P, HALVES, PAIR])
             )
             nc.vector.tensor_tensor(
-                out=products[i][:, k].rearrange("p b n (u e) -> p b n u e", u=HALVES),
+                out=products[i][:, k, samples[0] : samples[-1] + 1].rearrange("p b n (u e) -> p b n u e", u=HALVES),
                 in0=w_pairs,
                 in1=a_pairs,
                 op=MULT,
@@ -203,8 +202,9 @@ def tile_napl_conv_withsat_pb_s_kernel(tc, supports, cheb_2, spatial_attention, 
             nc.sync.dma_start(out=out_view[:, b, first : last + 1, :], in_=results[b][:, first : last + 1, :])
 
         load_weights(0, 0)
-        load_attention(0)
+        load_attention(0, slice(0, 1))
         load_weights(0, 1)
+        load_attention(0, slice(1, 2))
         for k in range(ORDERS):
             load_weights(1, k)
         load_attention(1)
@@ -223,57 +223,62 @@ def tile_napl_conv_withsat_pb_s_kernel(tc, supports, cheb_2, spatial_attention, 
         load_grad0(1)
 
         turn_weights(0, (0,), 0)
-        turn_attention(0, 1)
+        turn_attention(0, (0,), 1)
         turn_weights(0, (1,), 2)
+        turn_attention(0, (1,), 3)
         group_weights(0, (0,))
         group_weights(0, (1,))
-        multiply_turned(0, 0)
-        multiply_turned(0, 1)
+        multiply_turned(0, 0, (0,))
+        multiply_turned(0, 0, (1,))
+        multiply_turned(0, 1, (0,))
+        multiply_turned(0, 1, (1,))
         quantise_products(0, 0)
         quantise_products(0, 1)
-
-        turn_weights(1, (0, 1), 3)
-        turn_attention(1, 4)
+        turn_weights(1, (0, 1), 4)
+        turn_attention(1, (0, 1), 5)
         group_weights(1, (0, 1))
         regroup_grad(0, 0)
         multiply_turned(1, 0)
         multiply_turned(1, 1)
         quantise_products(1, 0)
-        quantise_products(1, 1)
         quantise_grad(0, 0)
-
-        turn_weights(2, (0, 1), 5)
-        turn_attention(2, 6)
+        quantise_products(1, 1)
+        turn_weights(2, (0, 1), 6)
+        turn_attention(2, (0, 1), 7)
         group_weights(2, (0, 1))
         regroup_grad(1, 0)
         regroup_grad(0, 1)
+        multiply(0, 0, 0)
+        multiply(1, 0, 0)
         multiply_turned(2, 0)
         multiply_turned(2, 1)
         quantise_products(2, 0)
-        quantise_products(2, 1)
         quantise_grad(1, 0)
+        quantise_products(2, 1)
         quantise_grad(0, 1)
-
-        turn_weights(3, (0, 1), 7)
-        turn_attention(3, 0)
+        turn_weights(3, (0, 1), 0)
+        turn_attention(3, (0, 1), 2)
         group_weights(3, (0, 1))
         regroup_grad(1, 1)
-        for k in range(ORDERS):
-            for i in range(ROW_TILES - 1):
-                multiply(i, 0, k)
-        for i in range(ROW_TILES - 1):
-            multiply(i, 1, 0)
+        multiply(0, 0, 1)
+        multiply(1, 0, 1)
+        multiply(2, 0, 0)
+        multiply(2, 0, 1)
+        multiply(0, 1, 0)
+        multiply(1, 1, 0)
+        multiply(2, 1, 0)
         multiply_turned(3, 0)
         multiply_turned(3, 1)
         quantise_products(3, 0)
         quantise_grad(1, 1)
         quantise_products(3, 1)
-        for b in range(BATCH):
-            multiply(3, b, 0)
-        for i in range(ROW_TILES - 1):
-            multiply(i, 1, 1)
-        for b in range(BATCH):
-            multiply(3, b, 1)
+        multiply(3, 0, 0)
+        multiply(3, 1, 0)
+        multiply(0, 1, 1)
+        multiply(1, 1, 1)
+        multiply(2, 1, 1)
+        multiply(3, 0, 1)
+        multiply(3, 1, 1)
         finish(0, 0)
         finish(1, 0)
         store(0, 0, 1)
@@ -284,6 +289,7 @@ def tile_napl_conv_withsat_pb_s_kernel(tc, supports, cheb_2, spatial_attention, 
         store(1, 0, 1)
         finish(2, 1)
         store(1, 2, 2)
-        for b in range(BATCH):
-            finish(3, b)
-            store(b, 3, 3)
+        finish(3, 0)
+        store(0, 3, 3)
+        finish(3, 1)
+        store(1, 3, 3)

@@ -19,6 +19,7 @@ CHANNELS = 256
 ORDERS = 2
 ROW_TILES = NODES // P
 PACK = 4
+GROUPS = ORDERS * BATCH
 HALVES = 2
 PAIR = 2
 GRAD_SLOTS = 5
@@ -59,16 +60,14 @@ def tile_napl_conv_withsat_pb_s_kernel(tc, supports, cheb_2, spatial_attention, 
         diagonal_bf16 = keep.tile([P, BATCH, 16], BF16)
         diagonal = keep.tile([P, BATCH, ROW_TILES], F32)
         weights_grouped = [keep.tile([P, ORDERS, P, HALVES], F32, name="w_grouped%d" % i) for i in range(ROW_TILES)]
-        products = [
-            keep.tile([P, ORDERS, BATCH, P, PACK], BF16, align_bytes=64, name="prod%d" % i) for i in range(ROW_TILES)
-        ]
+        products = [keep.tile([P, GROUPS, P, PACK], BF16, align_bytes=64, name="prod%d" % i) for i in range(ROW_TILES)]
         grads_grouped = {
             (k, b): keep.tile([P, CHANNELS, PACK], BF16, align_bytes=64, name="g_grouped%d%d" % (k, b))
             for k in range(ORDERS)
             for b in range(BATCH)
         }
-        prod_codes = keep.tile([P, ROW_TILES, ORDERS, BATCH * P], U32, align_bytes=64)
-        prod_scales = keep.tile([P, ROW_TILES, ORDERS, BATCH * P], U8, align_bytes=64)
+        prod_codes = keep.tile([P, ROW_TILES, GROUPS * P], U32, align_bytes=64)
+        prod_scales = keep.tile([P, ROW_TILES, GROUPS * P], U8, align_bytes=64)
         grad_codes = keep.tile([P, GRAD_SLOTS, CHANNELS], U32, align_bytes=64)
         grad_scales = keep.tile([P, GRAD_SLOTS, CHANNELS], U8, align_bytes=64)
         nc.gpsimd.memset(grad_codes[:, 0, :], 0)
@@ -107,6 +106,11 @@ def tile_napl_conv_withsat_pb_s_kernel(tc, supports, cheb_2, spatial_attention, 
                     )
             nc.gpsimd.tensor_copy(out=diagonal[:], in_=diagonal_bf16[:, :, 0:ROW_TILES])
 
+        def keep_clock_up(slot, matmuls):
+            unused = bank([P, P], slot)
+            for repeat in range(matmuls):
+                nc.tensor.matmul(unused[:], lhsT=identity[:], rhs=identity[:], start=True, stop=True)
+
         def turn_weights(i, orders, slot):
             words = weight_rows[i][:].rearrange("p k m -> p (k m)").bitcast(F32).rearrange("p (k w) -> p k w", k=ORDERS)
             turned = bank([P, len(orders), HALVES, P], slot)
@@ -121,7 +125,7 @@ def tile_napl_conv_withsat_pb_s_kernel(tc, supports, cheb_2, spatial_attention, 
             for j, b in enumerate(samples):
                 for u in range(HALVES):
                     nc.tensor.transpose(turned[:, u, j, :], words[:, b, u * P : (u + 1) * P], identity[:])
-            attention_turned[i, samples] = turned
+                attention_turned[i, b] = (turned, len(samples), j)
 
         def group_weights(i, orders):
             nc.scalar.copy(
@@ -129,12 +133,20 @@ def tile_napl_conv_withsat_pb_s_kernel(tc, supports, cheb_2, spatial_attention, 
                 in_=weights_turned[i, orders][:].rearrange("p k u n -> p k n u"),
             )
 
+        def group(i, k, b):
+            return ORDERS * b + k if i == ROW_TILES - 1 else BATCH * k + b
+
+        def groups(i, k, samples):
+            step = ORDERS if i == ROW_TILES - 1 else 1
+            return slice(group(i, k, samples[0]), group(i, k, samples[-1]) + 1, step)
+
         def multiply_turned(i, k, samples=(0, 1)):
+            turned, width, j = attention_turned[i, samples[0]]
             a_pairs = (
-                attention_turned[i, samples][:]
+                turned[:]
                 .rearrange("p u b n -> p (u b n)")
                 .bitcast(BF16)
-                .rearrange("p (u b n e) -> p b n u e", u=HALVES, b=len(samples), e=PAIR)
+                .rearrange("p (u b n e) -> p b n u e", u=HALVES, b=width, e=PAIR)[:, j : j + len(samples)]
             )
             w_pairs = (
                 weights_grouped[i][:, k]
@@ -145,17 +157,18 @@ def tile_napl_conv_withsat_pb_s_kernel(tc, supports, cheb_2, spatial_attention, 
                 .to_broadcast([P, len(samples), P, HALVES, PAIR])
             )
             nc.vector.tensor_tensor(
-                out=products[i][:, k, samples[0] : samples[-1] + 1].rearrange("p b n (u e) -> p b n u e", u=HALVES),
+                out=products[i][:, groups(i, k, samples)].rearrange("p b n (u e) -> p b n u e", u=HALVES),
                 in0=w_pairs,
                 in1=a_pairs,
                 op=MULT,
             )
 
-        def quantise_products(i, k):
+        def quantise_products(i, half):
+            columns = slice(half * 2 * P, (half + 1) * 2 * P)
             nc.vector.quantize_mx(
-                out=prod_codes[:, i, k, :].bitcast(E4M3_X4),
-                scales=prod_scales[:, i, k, :],
-                in_=products[i][:, k].rearrange("p b n t -> p (b n t)"),
+                out=prod_codes[:, i, columns].bitcast(E4M3_X4),
+                scales=prod_scales[:, i, columns],
+                in_=products[i][:, 2 * half : 2 * half + 2].rearrange("p g n t -> p (g n t)"),
             )
 
         def regroup_grad(k, b):
@@ -177,11 +190,11 @@ def tile_napl_conv_withsat_pb_s_kernel(tc, supports, cheb_2, spatial_attention, 
                 acc = bank([P, 2 * CHANNELS], SUM_BANK[i, b])
                 sums[i, b] = acc
             slot = GRAD_SLOT[k, b]
-            columns = slice(b * P, (b + 1) * P)
+            columns = slice(group(i, k, b) * P, (group(i, k, b) + 1) * P)
             nc.tensor.matmul_mx(
                 out=sums[i, b][:],
-                lhsT=prod_codes[:, i, k, columns].bitcast(E4M3_X4),
-                lhsT_scale=prod_scales[:, i, k, columns],
+                lhsT=prod_codes[:, i, columns].bitcast(E4M3_X4),
+                lhsT_scale=prod_scales[:, i, columns],
                 rhs=grad_codes[:, slot - 1 : slot + 1, :].rearrange("p s c -> p (s c)").bitcast(E5M2_X4),
                 rhs_scale=grad_scales[:, slot - 1 : slot + 1, :].rearrange("p s c -> p (s c)"),
                 start=(k == 0),
@@ -197,6 +210,18 @@ def tile_napl_conv_withsat_pb_s_kernel(tc, supports, cheb_2, spatial_attention, 
                 op0=MULT,
                 op1=ADD,
             )
+
+        def finish_on_gpsimd(i, b):
+            term = keep.tile([P, CHANNELS], F32, name="term%d%d" % (i, b))
+            nc.scalar.activation(
+                out=term[:],
+                in_=grad0[b][:, i, :],
+                func=mybir.ActivationFunctionType.Copy,
+                scale=diagonal[:, b, i : i + 1],
+            )
+            copied = keep.tile([P, CHANNELS], F32, name="copied%d%d" % (i, b))
+            nc.scalar.copy(out=copied[:], in_=sums[i, b][:, CHANNELS:])
+            nc.gpsimd.tensor_tensor(out=results[b][:, i, :], in0=term[:], in1=copied[:], op=ADD)
 
         def store(b, first, last):
             nc.sync.dma_start(out=out_view[:, b, first : last + 1, :], in_=results[b][:, first : last + 1, :])
@@ -257,6 +282,7 @@ def tile_napl_conv_withsat_pb_s_kernel(tc, supports, cheb_2, spatial_attention, 
         quantise_products(2, 1)
         quantise_grad(0, 1)
         turn_weights(3, (0, 1), 0)
+        keep_clock_up(2, 1)
         turn_attention(3, (0, 1), 2)
         group_weights(3, (0, 1))
         regroup_grad(1, 1)
@@ -267,29 +293,30 @@ def tile_napl_conv_withsat_pb_s_kernel(tc, supports, cheb_2, spatial_attention, 
         multiply(0, 1, 0)
         multiply(1, 1, 0)
         multiply(2, 1, 0)
-        multiply_turned(3, 0)
-        multiply_turned(3, 1)
+        multiply_turned(3, 0, (0,))
+        multiply_turned(3, 1, (0,))
+        multiply_turned(3, 0, (1,))
+        multiply_turned(3, 1, (1,))
         quantise_products(3, 0)
         quantise_grad(1, 1)
         quantise_products(3, 1)
         multiply(3, 0, 0)
-        multiply(3, 1, 0)
+        multiply(3, 0, 1)
         multiply(0, 1, 1)
         multiply(1, 1, 1)
         multiply(2, 1, 1)
-        multiply(3, 0, 1)
+        multiply(3, 1, 0)
         multiply(3, 1, 1)
         finish(0, 0)
+        store(0, 0, 0)
         finish(1, 0)
-        store(0, 0, 1)
-        finish(2, 0)
-        store(0, 2, 2)
+        store(0, 1, 1)
+        finish_on_gpsimd(2, 0)
+        finish(3, 0)
+        store(0, 2, 3)
         finish(0, 1)
         finish(1, 1)
         store(1, 0, 1)
         finish(2, 1)
-        store(1, 2, 2)
-        finish(3, 0)
-        store(0, 3, 3)
         finish(3, 1)
-        store(1, 3, 3)
+        store(1, 2, 3)

@@ -22,6 +22,7 @@ PACK = 4
 GROUPS = ORDERS * BATCH
 HALVES = 2
 PAIR = 2
+WINDOW = 16
 GRAD_SLOTS = 5
 GRAD_SLOT = {(0, 0): 1, (1, 0): 2, (0, 1): 3, (1, 1): 4}
 SUM_BANK = {(0, 0): 1, (1, 0): 3, (2, 0): 4, (0, 1): 5, (1, 1): 6, (2, 1): 7, (3, 0): 0, (3, 1): 2}
@@ -45,7 +46,16 @@ def tile_napl_conv_withsat_pb_s_kernel(tc, supports, cheb_2, spatial_attention, 
         grad_views = [
             grad_out[1 + k].rearrange("b (u p e) f t -> p b u (e f t)", u=HALVES, e=PAIR) for k in range(ORDERS)
         ]
-        flat_attention = spatial_attention.rearrange("b n m -> b (n m)")
+        flat_attention = spatial_attention.rearrange("b n m -> (b n m)")
+        steps = NODES * (NODES + 1)
+        diagonal_views = [
+            flat_attention[start : start + steps].rearrange("(p i w) -> p i w", i=ROW_TILES, w=NODES + 1)[:, :, columns]
+            for start, columns in (
+                (0, slice(0, WINDOW)),
+                (BATCH * NODES * NODES - steps, slice(NODES + 1 - WINDOW, NODES + 1)),
+            )
+        ]
+        diagonal_place = (0, WINDOW - 1)
         grad0_view = grad_out[0].rearrange("b (p i) f t -> p b (i f t)", i=ROW_TILES)
         out_view = out.rearrange("b (p i) f t -> p b i (f t)", i=ROW_TILES)
 
@@ -57,7 +67,7 @@ def tile_napl_conv_withsat_pb_s_kernel(tc, supports, cheb_2, spatial_attention, 
             for b in range(BATCH)
         }
         grad0 = [keep.tile([P, ROW_TILES, CHANNELS], BF16, name="grad0_%d" % b) for b in range(BATCH)]
-        diagonal_bf16 = keep.tile([P, BATCH, 16], BF16)
+        diagonal_windows = keep.tile([P, BATCH, ROW_TILES, WINDOW], BF16)
         diagonal = keep.tile([P, BATCH, ROW_TILES], F32)
         weights_grouped = [keep.tile([P, ORDERS, P, HALVES], F32, name="w_grouped%d" % i) for i in range(ROW_TILES)]
         products = [keep.tile([P, GROUPS, P, PACK], BF16, align_bytes=64, name="prod%d" % i) for i in range(ROW_TILES)]
@@ -97,14 +107,10 @@ def tile_napl_conv_withsat_pb_s_kernel(tc, supports, cheb_2, spatial_attention, 
         def load_grad0(b):
             nc.sync.dma_start(out=grad0[b][:].rearrange("p i c -> p (i c)"), in_=grad0_view[:, b])
 
-        def load_diagonal():
-            with nc.allow_non_contiguous_dma(reason="the diagonal is 1,024 single elements"):
-                for b in range(BATCH):
-                    nc.sync.dma_start(
-                        out=diagonal_bf16[:, b, 0:ROW_TILES],
-                        in_=flat_attention[b, 0 : NODES * NODES : NODES + 1].rearrange("(p i) -> p i", i=ROW_TILES),
-                    )
-            nc.gpsimd.tensor_copy(out=diagonal[:], in_=diagonal_bf16[:, :, 0:ROW_TILES])
+        def load_diagonal(b):
+            nc.sync.dma_start(out=diagonal_windows[:, b], in_=diagonal_views[b])
+            place = diagonal_place[b]
+            nc.gpsimd.tensor_copy(out=diagonal[:, b, :], in_=diagonal_windows[:, b, :, place])
 
         def keep_clock_up(slot, matmuls):
             unused = bank([P, P], slot)
@@ -243,8 +249,9 @@ def tile_napl_conv_withsat_pb_s_kernel(tc, supports, cheb_2, spatial_attention, 
             load_weights(3, k)
         load_attention(3)
         load_grad(1, 1)
-        load_diagonal()
+        load_diagonal(0)
         load_grad0(0)
+        load_diagonal(1)
         load_grad0(1)
 
         turn_weights(0, (0,), 0)

@@ -25,7 +25,7 @@ PAIR = 2
 WINDOW = 16
 GRAD_SLOTS = 5
 GRAD_SLOT = {(0, 0): 1, (1, 0): 2, (0, 1): 3, (1, 1): 4}
-SUM_BANK = {(0, 0): 1, (1, 0): 3, (2, 0): 4, (0, 1): 5, (1, 1): 6, (2, 1): 7, (3, 0): 0, (3, 1): 2}
+SUM_BANK = {(0, 0): 4, (1, 0): 5, (2, 0): 6, (0, 1): 7, (1, 1): 0, (2, 1): 2, (3, 0): 1, (3, 1): 3}
 
 FLOPS = 2 * ORDERS * BATCH * NODES * NODES * CHANNELS
 BYTES = 2 * (ORDERS * NODES * NODES + BATCH * NODES * NODES + 3 * BATCH * NODES * CHANNELS) + 4 * BATCH * NODES * CHANNELS
@@ -245,9 +245,10 @@ def tile_napl_conv_withsat_pb_s_kernel(tc, supports, cheb_2, spatial_attention, 
         load_attention(2)
         load_grad(1, 0)
         load_grad(0, 1)
-        for k in range(ORDERS):
-            load_weights(3, k)
-        load_attention(3)
+        load_weights(3, 0)
+        load_attention(3, slice(0, 1))
+        load_weights(3, 1)
+        load_attention(3, slice(1, 2))
         load_grad(1, 1)
         load_diagonal(0)
         load_grad0(0)
@@ -280,6 +281,7 @@ def tile_napl_conv_withsat_pb_s_kernel(tc, supports, cheb_2, spatial_attention, 
         group_weights(2, (0, 1))
         regroup_grad(1, 0)
         regroup_grad(0, 1)
+        keep_clock_up(0, 1)
         multiply(0, 0, 0)
         multiply(1, 0, 0)
         multiply_turned(2, 0)
@@ -288,23 +290,25 @@ def tile_napl_conv_withsat_pb_s_kernel(tc, supports, cheb_2, spatial_attention, 
         quantise_grad(1, 0)
         quantise_products(2, 1)
         quantise_grad(0, 1)
-        turn_weights(3, (0, 1), 0)
-        keep_clock_up(2, 1)
-        turn_attention(3, (0, 1), 2)
-        group_weights(3, (0, 1))
+        turn_weights(3, (0,), 0)
+        turn_attention(3, (0,), 1)
+        turn_weights(3, (1,), 2)
+        turn_attention(3, (1,), 3)
+        group_weights(3, (0,))
+        group_weights(3, (1,))
         regroup_grad(1, 1)
+        multiply_turned(3, 0, (0,))
+        multiply_turned(3, 1, (0,))
+        multiply_turned(3, 0, (1,))
+        quantise_products(3, 0)
+        multiply_turned(3, 1, (1,))
+        multiply(2, 0, 0)
         multiply(0, 0, 1)
         multiply(1, 0, 1)
-        multiply(2, 0, 0)
         multiply(2, 0, 1)
         multiply(0, 1, 0)
         multiply(1, 1, 0)
         multiply(2, 1, 0)
-        multiply_turned(3, 0, (0,))
-        multiply_turned(3, 1, (0,))
-        multiply_turned(3, 0, (1,))
-        multiply_turned(3, 1, (1,))
-        quantise_products(3, 0)
         quantise_grad(1, 1)
         quantise_products(3, 1)
         multiply(3, 0, 0)
@@ -325,5 +329,6 @@ def tile_napl_conv_withsat_pb_s_kernel(tc, supports, cheb_2, spatial_attention, 
         finish(1, 1)
         store(1, 0, 1)
         finish(2, 1)
+        store(1, 2, 2)
         finish(3, 1)
-        store(1, 2, 3)
+        store(1, 3, 3)

from contextlib import ExitStack

import concourse.mybir as mybir
from concourse.masks import make_identity

BF16 = mybir.dt.bfloat16
F32 = mybir.dt.float32
U32 = mybir.dt.uint32
U8 = mybir.dt.uint8
E4M3_X4 = mybir.dt.float8_e4m3fn_x4
E5M2_X4 = mybir.dt.float8_e5m2_x4
MULT = mybir.AluOpType.mult
ADD = mybir.AluOpType.add

P = 128
BATCH = 2
NODES = 512
CHANNELS = 256
ORDERS = 2
ROW_TILES = NODES // P
PACK = 4
GROUPS = ORDERS * BATCH
HALVES = 2
PAIR = 2
WINDOW = 16
GRAD_SLOTS = 5
GRAD_SLOT = {(0, 0): 1, (1, 0): 2, (0, 1): 3, (1, 1): 4}
SUM_BANK = {(0, 0): 4, (1, 0): 5, (2, 0): 6, (0, 1): 7, (1, 1): 0, (2, 1): 2, (3, 0): 1, (3, 1): 3}

FLOPS = 2 * ORDERS * BATCH * NODES * NODES * CHANNELS
BYTES = 2 * (ORDERS * NODES * NODES + BATCH * NODES * NODES + 3 * BATCH * NODES * CHANNELS) + 4 * BATCH * NODES * CHANNELS


def tile_napl_conv_withsat_pb_s_kernel(tc, supports, cheb_2, spatial_attention, x, grad_out, out):
    nc = tc.nc
    with ExitStack() as ctx:
        keep = ctx.enter_context(tc.tile_pool(name="keep", bufs=1))
        banks = ctx.enter_context(tc.psum_pool(name="banks", bufs=1))
        ctx.enter_context(tc.manual_schedule())

        identity = keep.tile([P, P], F32)
        make_identity(nc, identity[:])

        weight_views = [w.rearrange("(p i) m -> p i m", i=ROW_TILES) for w in (supports, cheb_2)]
        attention_view = spatial_attention.rearrange("b (p i) m -> p b i m", i=ROW_TILES)
        grad_views = [
            grad_out[1 + k].rearrange("b (u p e) f t -> p b u (e f t)", u=HALVES, e=PAIR) for k in range(ORDERS)
        ]
        flat_attention = spatial_attention.rearrange("b n m -> (b n m)")
        steps = NODES * (NODES + 1)
        diagonal_views = [
            flat_attention[start : start + steps].rearrange("(p i w) -> p i w", i=ROW_TILES, w=NODES + 1)[:, :, columns]
            for start, columns in (
                (0, slice(0, WINDOW)),
                (BATCH * NODES * NODES - steps, slice(NODES + 1 - WINDOW, NODES + 1)),
            )
        ]
        diagonal_place = (0, WINDOW - 1)
        grad0_view = grad_out[0].rearrange("b (p i) f t -> p b (i f t)", i=ROW_TILES)
        out_view = out.rearrange("b (p i) f t -> p b i (f t)", i=ROW_TILES)

        weight_rows = [keep.tile([P, ORDERS, NODES], BF16, name="w_rows%d" % i) for i in range(ROW_TILES)]
        attention_rows = [keep.tile([P, BATCH, NODES], BF16, name="a_rows%d" % i) for i in range(ROW_TILES)]
        grad_raw = {
            (k, b): keep.tile([P, PACK, CHANNELS], BF16, name="g_raw%d%d" % (k, b))
            for k in range(ORDERS)
            for b in range(BATCH)
        }
        grad0 = [keep.tile([P, ROW_TILES, CHANNELS], BF16, name="grad0_%d" % b) for b in range(BATCH)]
        diagonal_windows = keep.tile([P, BATCH, ROW_TILES, WINDOW], BF16)
        diagonal = keep.tile([P, BATCH, ROW_TILES], F32)
        weights_grouped = [keep.tile([P, ORDERS, P, HALVES], F32, name="w_grouped%d" % i) for i in range(ROW_TILES)]
        products = [keep.tile([P, GROUPS, P, PACK], BF16, align_bytes=64, name="prod%d" % i) for i in range(ROW_TILES)]
        grads_grouped = {
            (k, b): keep.tile([P, CHANNELS, PACK], BF16, align_bytes=64, name="g_grouped%d%d" % (k, b))
            for k in range(ORDERS)
            for b in range(BATCH)
        }
        prod_codes = keep.tile([P, ROW_TILES, GROUPS * P], U32, align_bytes=64)
        prod_scales = keep.tile([P, ROW_TILES, GROUPS * P], U8, align_bytes=64)
        grad_codes = keep.tile([P, GRAD_SLOTS, CHANNELS], U32, align_bytes=64)
        grad_scales = keep.tile([P, GRAD_SLOTS, CHANNELS], U8, align_bytes=64)
        nc.gpsimd.memset(grad_codes[:, 0, :], 0)
        nc.gpsimd.memset(grad_scales[:, 0, :], 0)
        weights_turned = {}
        attention_turned = {}
        sums = {}
        results = [
            keep.tile([P, ROW_TILES, CHANNELS], F32, name="result%d" % b) for b in range(BATCH)
        ]

        def bank(shape, slot):
            return banks.tile(shape, F32, tag="bank%d" % slot, name="in_bank%d" % slot)

        def load_weights(i, k):
            nc.sync.dma_start(out=weight_rows[i][:, k, :], in_=weight_views[k][:, i, :])

        def load_attention(i, samples=slice(0, BATCH)):
            nc.sync.dma_start(out=attention_rows[i][:, samples], in_=attention_view[:, samples, i, :])

        def load_grad(k, b):
            nc.sync.dma_start(
                out=grad_raw[k, b][:].rearrange("p (u e) c -> p u (e c)", u=HALVES),
                in_=grad_views[k][:, b],
            )

        def load_grad0(b):
            nc.sync.dma_start(out=grad0[b][:].rearrange("p i c -> p (i c)"), in_=grad0_view[:, b])

        def load_diagonal(b):
            nc.sync.dma_start(out=diagonal_windows[:, b], in_=diagonal_views[b])
            place = diagonal_place[b]
            nc.gpsimd.tensor_copy(out=diagonal[:, b, :], in_=diagonal_windows[:, b, :, place])

        def keep_clock_up(slot, matmuls):
            unused = bank([P, P], slot)
            for repeat in range(matmuls):
                nc.tensor.matmul(unused[:], lhsT=identity[:], rhs=identity[:], start=True, stop=True)

        def turn_weights(i, orders, slot):
            words = weight_rows[i][:].rearrange("p k m -> p (k m)").bitcast(F32).rearrange("p (k w) -> p k w", k=ORDERS)
            turned = bank([P, len(orders), HALVES, P], slot)
            for j, k in enumerate(orders):
                for u in range(HALVES):
                    nc.tensor.transpose(turned[:, j, u, :], words[:, k, u * P : (u + 1) * P], identity[:])
            weights_turned[i, orders] = turned

        def turn_attention(i, samples, slot):
            words = attention_rows[i][:].rearrange("p b m -> p (b m)").bitcast(F32).rearrange("p (b w) -> p b w", b=BATCH)
            turned = bank([P, HALVES, len(samples), P], slot)
            for j, b in enumerate(samples):
                for u in range(HALVES):
                    nc.tensor.transpose(turned[:, u, j, :], words[:, b, u * P : (u + 1) * P], identity[:])
                attention_turned[i, b] = (turned, len(samples), j)

        def group_weights(i, orders):
            nc.scalar.copy(
                out=weights_grouped[i][:, orders[0] : orders[-1] + 1],
                in_=weights_turned[i, orders][:].rearrange("p k u n -> p k n u"),
            )

        def group(i, k, b):
            return ORDERS * b + k if i == ROW_TILES - 1 else BATCH * k + b

        def groups(i, k, samples):
            step = ORDERS if i == ROW_TILES - 1 else 1
            return slice(group(i, k, samples[0]), group(i, k, samples[-1]) + 1, step)

        def multiply_turned(i, k, samples=(0, 1)):
            turned, width, j = attention_turned[i, samples[0]]
            a_pairs = (
                turned[:]
                .rearrange("p u b n -> p (u b n)")
                .bitcast(BF16)
                .rearrange("p (u b n e) -> p b n u e", u=HALVES, b=width, e=PAIR)[:, j : j + len(samples)]
            )
            w_pairs = (
                weights_grouped[i][:, k]
                .rearrange("p n u -> p (n u)")
                .bitcast(BF16)
                .rearrange("p (n u e) -> p n u e", u=HALVES, e=PAIR)
                .unsqueeze(1)
                .to_broadcast([P, len(samples), P, HALVES, PAIR])
            )
            nc.vector.tensor_tensor(
                out=products[i][:, groups(i, k, samples)].rearrange("p b n (u e) -> p b n u e", u=HALVES),
                in0=w_pairs,
                in1=a_pairs,
                op=MULT,
            )

        def quantise_products(i, half):
            columns = slice(half * 2 * P, (half + 1) * 2 * P)
            nc.vector.quantize_mx(
                out=prod_codes[:, i, columns].bitcast(E4M3_X4),
                scales=prod_scales[:, i, columns],
                in_=products[i][:, 2 * half : 2 * half + 2].rearrange("p g n t -> p (g n t)"),
            )

        def regroup_grad(k, b):
            nc.scalar.copy(
                out=grads_grouped[k, b][:].rearrange("p (c r) t -> p c t r", r=4),
                in_=grad_raw[k, b][:].rearrange("p t (c r) -> p c t r", r=4),
            )

        def quantise_grad(k, b):
            slot = GRAD_SLOT[k, b]
            nc.vector.quantize_mx(
                out=grad_codes[:, slot, :].bitcast(E5M2_X4),
                scales=grad_scales[:, slot, :],
                in_=grads_grouped[k, b][:].rearrange("p c t -> p (c t)"),
            )

        def multiply(i, b, k):
            if k == 0:
                acc = bank([P, 2 * CHANNELS], SUM_BANK[i, b])
                sums[i, b] = acc
            slot = GRAD_SLOT[k, b]
            columns = slice(group(i, k, b) * P, (group(i, k, b) + 1) * P)
            nc.tensor.matmul_mx(
                out=sums[i, b][:],
                lhsT=prod_codes[:, i, columns].bitcast(E4M3_X4),
                lhsT_scale=prod_scales[:, i, columns],
                rhs=grad_codes[:, slot - 1 : slot + 1, :].rearrange("p s c -> p (s c)").bitcast(E5M2_X4),
                rhs_scale=grad_scales[:, slot - 1 : slot + 1, :].rearrange("p s c -> p (s c)"),
                start=(k == 0),
                stop=(k == ORDERS - 1),
            )

        def finish(i, b):
            nc.vector.scalar_tensor_tensor(
                out=results[b][:, i, :],
                in0=grad0[b][:, i, :],
                scalar=diagonal[:, b, i : i + 1],
                in1=sums[i, b][:, CHANNELS:],
                op0=MULT,
                op1=ADD,
            )

        def finish_on_gpsimd(i, b):
            term = keep.tile([P, CHANNELS], F32, name="term%d%d" % (i, b))
            nc.scalar.activation(
                out=term[:],
                in_=grad0[b][:, i, :],
                func=mybir.ActivationFunctionType.Copy,
                scale=diagonal[:, b, i : i + 1],
            )
            copied = keep.tile([P, CHANNELS], F32, name="copied%d%d" % (i, b))
            nc.scalar.copy(out=copied[:], in_=sums[i, b][:, CHANNELS:])
            nc.gpsimd.tensor_tensor(out=results[b][:, i, :], in0=term[:], in1=copied[:], op=ADD)

        def store(b, first, last):
            nc.sync.dma_start(out=out_view[:, b, first : last + 1, :], in_=results[b][:, first : last + 1, :])

        load_weights(0, 0)
        load_attention(0, slice(0, 1))
        load_weights(0, 1)
        load_attention(0, slice(1, 2))
        for k in range(ORDERS):
            load_weights(1, k)
        load_attention(1)
        load_grad(0, 0)
        for k in range(ORDERS):
            load_weights(2, k)
        load_attention(2)
        load_grad(1, 0)
        load_grad(0, 1)
        load_weights(3, 0)
        load_attention(3, slice(0, 1))
        load_weights(3, 1)
        load_attention(3, slice(1, 2))
        load_grad(1, 1)
        load_diagonal(0)
        load_grad0(0)
        load_diagonal(1)
        load_grad0(1)

        turn_weights(0, (0,), 0)
        turn_attention(0, (0,), 1)
        turn_weights(0, (1,), 2)
        turn_attention(0, (1,), 3)
        group_weights(0, (0,))
        group_weights(0, (1,))
        multiply_turned(0, 0, (0,))
        multiply_turned(0, 0, (1,))
        multiply_turned(0, 1, (0,))
        multiply_turned(0, 1, (1,))
        quantise_products(0, 0)
        quantise_products(0, 1)
        turn_weights(1, (0, 1), 4)
        turn_attention(1, (0, 1), 5)
        group_weights(1, (0, 1))
        regroup_grad(0, 0)
        multiply_turned(1, 0)
        multiply_turned(1, 1)
        quantise_products(1, 0)
        quantise_grad(0, 0)
        quantise_products(1, 1)
        turn_weights(2, (0, 1), 6)
        turn_attention(2, (0, 1), 7)
        group_weights(2, (0, 1))
        regroup_grad(1, 0)
        regroup_grad(0, 1)
        keep_clock_up(0, 1)
        multiply(0, 0, 0)
        multiply(1, 0, 0)
        multiply_turned(2, 0)
        multiply_turned(2, 1)
        quantise_products(2, 0)
        quantise_grad(1, 0)
        quantise_products(2, 1)
        quantise_grad(0, 1)
        turn_weights(3, (0,), 0)
        turn_attention(3, (0,), 1)
        turn_weights(3, (1,), 2)
        turn_attention(3, (1,), 3)
        group_weights(3, (0,))
        group_weights(3, (1,))
        regroup_grad(1, 1)
        multiply_turned(3, 0, (0,))
        multiply_turned(3, 1, (0,))
        multiply_turned(3, 0, (1,))
        quantise_products(3, 0)
        multiply_turned(3, 1, (1,))
        multiply(2, 0, 0)
        multiply(0, 0, 1)
        multiply(1, 0, 1)
        multiply(2, 0, 1)
        multiply(0, 1, 0)
        multiply(1, 1, 0)
        multiply(2, 1, 0)
        quantise_grad(1, 1)
        quantise_products(3, 1)
        multiply(3, 0, 0)
        multiply(3, 0, 1)
        multiply(0, 1, 1)
        multiply(1, 1, 1)
        multiply(2, 1, 1)
        multiply(3, 1, 0)
        multiply(3, 1, 1)
        finish(0, 0)
        store(0, 0, 0)
        finish(1, 0)
        store(0, 1, 1)
        finish_on_gpsimd(2, 0)
        finish(3, 0)
        store(0, 2, 3)
        finish(0, 1)
        finish(1, 1)
        store(1, 0, 1)
        finish(2, 1)
        store(1, 2, 2)
        finish(3, 1)
        store(1, 3, 3)
